import numpy as np
import ml_dtypes


def mxq(x, axis, fmt="e4m3"):
    dtype, down = {"e4m3": (ml_dtypes.float8_e4m3fn, 7), "e5m2": (ml_dtypes.float8_e5m2, 14)}[fmt]
    v = np.moveaxis(np.asarray(x, np.float32).astype(ml_dtypes.bfloat16).astype(np.float64), axis, -1)
    blocks = v.reshape(v.shape[:-1] + (-1, 32))
    amax = np.abs(blocks).max(-1, keepdims=True)
    byte = np.maximum(np.where(amax > 0, np.frexp(amax)[1] - 1 + 127, 0) - down, 1)
    scale = np.exp2(byte - 127.0)
    codes = (blocks / scale).astype(np.float32).astype(dtype).astype(np.float64)
    return np.moveaxis((codes * scale).reshape(v.shape), -1, axis)


WIDE = False


def mx_kscale(k):
    if not WIDE:
        return np.ones(k)
    levels = np.array([10, -10, 5, -5, 0])
    a = np.random.permutation(np.resize(levels, k // 512 * 4)).reshape(k // 512, 4)
    idx = np.arange(k)
    return np.exp2(a[idx // 512, idx % 128 // 32])


BF16 = ml_dtypes.bfloat16


def bf(x):
    return np.asarray(x, np.float32).astype(BF16)


def f64(x):
    return np.asarray(x).astype(np.float64)


B, S, I0, I1, I2, I3, I4, O0, O1, O2, O3, O4, R1, R2, R3, R4 = 2, 256, 4, 2, 2, 2, 16, 4, 4, 2, 2, 32, 16, 512, 512, 128
IA, OA = I0 * I1, O0 * O1


def tt_step(t, c):
    I, O, r = t.shape
    _, i, o, q = c.shape
    p = mxq(t.reshape(I * O, r), 1, "e4m3") @ mxq(c.reshape(r, i * o * q), 0, "e4m3")
    return p.reshape(I, O, i, o, q).transpose(0, 2, 1, 3, 4).reshape(I * i, O * o, q)


def setup_inputs():
    s, u = mx_kscale(R2), mx_kscale(R3)
    return {"t1": bf(np.random.standard_normal((IA, OA, R2)) * s),
            "core2": bf(np.random.standard_normal((R2, I2, O2, R3)) / np.sqrt(R2) / s[:, None, None, None] * u),
            "core3": bf(np.random.standard_normal((R3, I3, O3, R4)) / np.sqrt(R3) / u[:, None, None, None])}


def reference(t1, core2, core3):
    t2 = tt_step(f64(t1), f64(core2))
    return tt_step(t2, f64(core3))

@@ -1,0 +1,142 @@
+from contextlib import ExitStack
+
+import concourse.mybir as mybir
+from concourse.masks import make_identity
+
+BF16 = mybir.dt.bfloat16
+F32 = mybir.dt.float32
+U32 = mybir.dt.uint32
+U8 = mybir.dt.uint8
+FP8X4 = mybir.dt.float8_e4m3fn_x4
+
+P = 128
+PACK = 4
+BOND = P * PACK
+N_I, N_O = 8, 16
+PAIRS = 4
+OUT_COLS = 512
+VECTOR_COLS = 384
+
+FLOPS = 2 * 128 * 512 * 2048 + 2 * 512 * 512 * 512
+
+
+def regroup(nc, grouped, raw):
+    for copy, cols in (
+        (nc.vector.tensor_copy, slice(0, VECTOR_COLS)),
+        (nc.scalar.copy, slice(VECTOR_COLS, 512)),
+    ):
+        copy(
+            out=grouped[:, cols, :].rearrange("p (c n) j -> p c j n", n=4),
+            in_=raw[:, :, cols].rearrange("p j (c n) -> p c j n", n=4),
+        )
+
+
+def quantise(nc, codes, scales, grouped):
+    nc.vector.quantize_mx(
+        out=codes[:].bitcast(FP8X4),
+        scales=scales[:],
+        in_=grouped[:].rearrange("p w j -> p (w j)"),
+    )
+
+
+def tile_linear2mpo_pa_s_kernel(tc, t1, core2, core3, out):
+    nc = tc.nc
+    with ExitStack() as ctx:
+        keep = ctx.enter_context(tc.tile_pool(name="keep", bufs=1))
+        bank_t1 = ctx.enter_context(tc.psum_pool(name="bank_t1", bufs=1))
+        bank_t2 = ctx.enter_context(tc.psum_pool(name="bank_t2", bufs=4))
+        bank_out = ctx.enter_context(tc.psum_pool(name="bank_out", bufs=3))
+
+        core2_view = core2.rearrange("(p j) i o q -> (i o) p j q", j=PACK)
+        core3_view = core3.rearrange("(t p) a b s -> p t (a b s)", p=P)
+        t1_rows = keep.tile([P, BOND], BF16)
+        nc.scalar.dma_start(out=t1_rows[:], in_=t1.rearrange("i o r -> (i o) r"))
+        raw2 = [keep.tile([P, PACK, BOND], BF16, name="raw2_%d" % c) for c in range(PAIRS)]
+        raw3 = keep.tile([P, PACK, OUT_COLS], BF16)
+        nc.sync.dma_start(out=raw2[0][:], in_=core2_view[0])
+        nc.sync.dma_start(out=raw2[1][:], in_=core2_view[1])
+        nc.sync.dma_start(out=raw3[:], in_=core3_view)
+        nc.sync.dma_start(out=raw2[2][:], in_=core2_view[2])
+        nc.sync.dma_start(out=raw2[3][:], in_=core2_view[3])
+
+        identity = keep.tile([P, P], F32)
+        make_identity(nc, identity[:])
+        t1_words = t1_rows[:].bitcast(F32).rearrange("c (p u) -> c u p", u=2)
+        t1_T = bank_t1.tile([P, 2, P], F32)
+        for u in range(2):
+            nc.tensor.transpose(t1_T[:, u, :], t1_words[:, u, :], identity[:])
+        t1_grouped = keep.tile([P, P, PACK], BF16, align_bytes=64)
+        nc.scalar.copy(
+            out=t1_grouped[:]
+            .rearrange("p w j -> p (w j)")
+            .bitcast(F32)
+            .rearrange("p (o i u) -> p o i u", o=N_O, i=N_I),
+            in_=t1_T[:].rearrange("p u (i o) -> p o i u", i=N_I),
+        )
+        t1_codes = keep.tile([P, P], U32, align_bytes=64)
+        t1_scales = keep.tile([P, P], U8, align_bytes=64)
+        quantise(nc, t1_codes, t1_scales, t1_grouped)
+
+        grouped3 = keep.tile([P, OUT_COLS, PACK], BF16, align_bytes=64)
+        codes3 = keep.tile([P, OUT_COLS], U32, align_bytes=64)
+        scales3 = keep.tile([P, OUT_COLS], U8, align_bytes=64)
+
+        out_view = out.rearrange(
+            "(I i a) (O o b) s -> i o a O I (b s)", I=N_I, i=2, a=2, O=N_O, o=2, b=2
+        )
+
+        t2_codes = []
+        t2_scales = []
+
+        def step1(c):
+            grouped2 = keep.tile([P, BOND, PACK], BF16, name="grouped2_%d" % c, align_bytes=64)
+            codes2 = keep.tile([P, BOND], U32, name="codes2_%d" % c, align_bytes=64)
+            scales2 = keep.tile([P, BOND], U8, name="scales2_%d" % c, align_bytes=64)
+            regroup(nc, grouped2, raw2[c])
+            quantise(nc, codes2, scales2, grouped2)
+            t2_T = bank_t2.tile([P, PACK, P], F32)
+            for t in range(PACK):
+                cols = slice(t * P, (t + 1) * P)
+                nc.tensor.matmul_mx(
+                    out=t2_T[:, t, :],
+                    lhsT=codes2[:, cols].bitcast(FP8X4),
+                    lhsT_scale=scales2[:, cols],
+                    rhs=t1_codes[:].bitcast(FP8X4),
+                    rhs_scale=t1_scales[:],
+                    start=True,
+                    stop=True,
+                )
+            t2_grouped = keep.tile([P, P, PACK], BF16, name="t2_grouped_%d" % c, align_bytes=64)
+            nc.scalar.copy(out=t2_grouped[:], in_=t2_T[:].rearrange("p t w -> p w t"))
+            codes = keep.tile([P, P], U32, name="t2_codes_%d" % c, align_bytes=64)
+            scales = keep.tile([P, P], U8, name="t2_scales_%d" % c, align_bytes=64)
+            quantise(nc, codes, scales, t2_grouped)
+            t2_codes.append(codes)
+            t2_scales.append(scales)
+
+        def step2(c):
+            acc = bank_out.tile([P, OUT_COLS], F32)
+            nc.tensor.matmul_mx(
+                out=acc[:],
+                lhsT=t2_codes[c][:].bitcast(FP8X4),
+                lhsT_scale=t2_scales[c][:],
+                rhs=codes3[:].bitcast(FP8X4),
+                rhs_scale=scales3[:],
+                start=True,
+                stop=True,
+            )
+            result = keep.tile([P, OUT_COLS], F32, name="result_%d" % c)
+            nc.scalar.copy(out=result[:], in_=acc[:])
+            for a in range(2):
+                nc.sync.dma_start(out=out_view[c // 2, c % 2, a], in_=result[:, a * 256 : (a + 1) * 256])
+
+        step1(0)
+        step1(1)
+        regroup(nc, grouped3, raw3)
+        quantise(nc, codes3, scales3, grouped3)
+        step2(0)
+        step2(1)
+        step1(2)
+        step2(2)
+        step1(3)
+        step2(3)

@@ -15,15 +15,18 @@ BOND = P * PACK
 N_I, N_O = 8, 16
 PAIRS = 4
 OUT_COLS = 512
-VECTOR_COLS = 384
 
 FLOPS = 2 * 128 * 512 * 2048 + 2 * 512 * 512 * 512
 
+VECTOR_EIGHTHS = 6
+HALF = 256
 
-def regroup(nc, grouped, raw):
+
+def regroup(nc, grouped, raw, first, count):
+    split = first + count * VECTOR_EIGHTHS // 8
     for copy, cols in (
-        (nc.vector.tensor_copy, slice(0, VECTOR_COLS)),
-        (nc.scalar.copy, slice(VECTOR_COLS, 512)),
+        (nc.vector.tensor_copy, slice(first, split)),
+        (nc.scalar.copy, slice(split, first + count)),
     ):
         copy(
             out=grouped[:, cols, :].rearrange("p (c n) j -> p c j n", n=4),
@@ -33,36 +36,47 @@ def regroup(nc, grouped, raw):
 
 def quantise(nc, codes, scales, grouped):
     nc.vector.quantize_mx(
-        out=codes[:].bitcast(FP8X4),
-        scales=scales[:],
-        in_=grouped[:].rearrange("p w j -> p (w j)"),
+        out=codes.bitcast(FP8X4),
+        scales=scales,
+        in_=grouped.rearrange("p w j -> p (w j)"),
     )
 
 
 def tile_linear2mpo_pa_s_kernel(tc, t1, core2, core3, out):
     nc = tc.nc
     with ExitStack() as ctx:
+        ctx.enter_context(tc.manual_schedule())
         keep = ctx.enter_context(tc.tile_pool(name="keep", bufs=1))
-        bank_t1 = ctx.enter_context(tc.psum_pool(name="bank_t1", bufs=1))
-        bank_t2 = ctx.enter_context(tc.psum_pool(name="bank_t2", bufs=4))
-        bank_out = ctx.enter_context(tc.psum_pool(name="bank_out", bufs=3))
+        bank_t2 = ctx.enter_context(tc.psum_pool(name="bank_t2", bufs=2))
+        bank_out = ctx.enter_context(tc.psum_pool(name="bank_out", bufs=6))
 
         core2_view = core2.rearrange("(p j) i o q -> (i o) p j q", j=PACK)
         core3_view = core3.rearrange("(t p) a b s -> p t (a b s)", p=P)
         t1_rows = keep.tile([P, BOND], BF16)
         nc.scalar.dma_start(out=t1_rows[:], in_=t1.rearrange("i o r -> (i o) r"))
-        raw2 = [keep.tile([P, PACK, BOND], BF16, name="raw2_%d" % c) for c in range(PAIRS)]
-        raw3 = keep.tile([P, PACK, OUT_COLS], BF16)
-        nc.sync.dma_start(out=raw2[0][:], in_=core2_view[0])
-        nc.sync.dma_start(out=raw2[1][:], in_=core2_view[1])
-        nc.sync.dma_start(out=raw3[:], in_=core3_view)
-        nc.sync.dma_start(out=raw2[2][:], in_=core2_view[2])
-        nc.sync.dma_start(out=raw2[3][:], in_=core2_view[3])
+        raw = [keep.tile([P, PACK, BOND], BF16, name="raw_%d" % c) for c in range(PAIRS + 1)]
+        for c in range(PAIRS):
+            nc.sync.dma_start(out=raw[c][:], in_=core2_view[c])
+        nc.sync.dma_start(out=raw[PAIRS][:], in_=core3_view)
+
+        grouped = [
+            keep.tile([P, BOND, PACK], BF16, name="grouped_%d" % c, align_bytes=64)
+            for c in range(PAIRS + 1)
+        ]
+        codes = [keep.tile([P, BOND], U32, name="codes_%d" % c, align_bytes=64) for c in range(PAIRS + 1)]
+        scales = [keep.tile([P, BOND], U8, name="scales_%d" % c, align_bytes=64) for c in range(PAIRS + 1)]
+        t2_grouped = [
+            keep.tile([P, P, PACK], BF16, name="t2_grouped_%d" % c, align_bytes=64) for c in range(PAIRS)
+        ]
+        t2_codes = [keep.tile([P, P], U32, name="t2_codes_%d" % c, align_bytes=64) for c in range(PAIRS)]
+        t2_scales = [keep.tile([P, P], U8, name="t2_scales_%d" % c, align_bytes=64) for c in range(PAIRS)]
+
+        regroup(nc, grouped[0], raw[0], 0, BOND)
 
         identity = keep.tile([P, P], F32)
         make_identity(nc, identity[:])
         t1_words = t1_rows[:].bitcast(F32).rearrange("c (p u) -> c u p", u=2)
-        t1_T = bank_t1.tile([P, 2, P], F32)
+        t1_T = bank_t2.tile([P, 2, P], F32, tag="t2_T")
         for u in range(2):
             nc.tensor.transpose(t1_T[:, u, :], t1_words[:, u, :], identity[:])
         t1_grouped = keep.tile([P, P, PACK], BF16, align_bytes=64)
@@ -75,68 +89,50 @@ def tile_linear2mpo_pa_s_kernel(tc, t1, core2, core3, out):
         )
         t1_codes = keep.tile([P, P], U32, align_bytes=64)
         t1_scales = keep.tile([P, P], U8, align_bytes=64)
-        quantise(nc, t1_codes, t1_scales, t1_grouped)
 
-        grouped3 = keep.tile([P, OUT_COLS, PACK], BF16, align_bytes=64)
-        codes3 = keep.tile([P, OUT_COLS], U32, align_bytes=64)
-        scales3 = keep.tile([P, OUT_COLS], U8, align_bytes=64)
-
-        out_view = out.rearrange(
-            "(I i a) (O o b) s -> i o a O I (b s)", I=N_I, i=2, a=2, O=N_O, o=2, b=2
-        )
-
-        t2_codes = []
-        t2_scales = []
-
-        def step1(c):
-            grouped2 = keep.tile([P, BOND, PACK], BF16, name="grouped2_%d" % c, align_bytes=64)
-            codes2 = keep.tile([P, BOND], U32, name="codes2_%d" % c, align_bytes=64)
-            scales2 = keep.tile([P, BOND], U8, name="scales2_%d" % c, align_bytes=64)
-            regroup(nc, grouped2, raw2[c])
-            quantise(nc, codes2, scales2, grouped2)
-            t2_T = bank_t2.tile([P, PACK, P], F32)
+        for c in range(PAIRS):
+            quantise(nc, codes[c][:], scales[c][:], grouped[c][:])
+            if c == 0:
+                quantise(nc, t1_codes[:], t1_scales[:], t1_grouped[:])
+            t2_T = bank_t2.tile([P, PACK, P], F32, tag="t2_T")
             for t in range(PACK):
                 cols = slice(t * P, (t + 1) * P)
                 nc.tensor.matmul_mx(
                     out=t2_T[:, t, :],
-                    lhsT=codes2[:, cols].bitcast(FP8X4),
-                    lhsT_scale=scales2[:, cols],
+                    lhsT=codes[c][:, cols].bitcast(FP8X4),
+                    lhsT_scale=scales[c][:, cols],
                     rhs=t1_codes[:].bitcast(FP8X4),
                     rhs_scale=t1_scales[:],
                     start=True,
                     stop=True,
                 )
-            t2_grouped = keep.tile([P, P, PACK], BF16, name="t2_grouped_%d" % c, align_bytes=64)
-            nc.scalar.copy(out=t2_grouped[:], in_=t2_T[:].rearrange("p t w -> p w t"))
-            codes = keep.tile([P, P], U32, name="t2_codes_%d" % c, align_bytes=64)
-            scales = keep.tile([P, P], U8, name="t2_scales_%d" % c, align_bytes=64)
-            quantise(nc, codes, scales, t2_grouped)
-            t2_codes.append(codes)
-            t2_scales.append(scales)
+            regroup(nc, grouped[c + 1], raw[c + 1], 0, BOND if c + 1 < PAIRS else HALF)
+            nc.scalar.copy(out=t2_grouped[c][:], in_=t2_T[:].rearrange("p t w -> p w t"))
+            if c > 0:
+                quantise(nc, t2_codes[c - 1][:], t2_scales[c - 1][:], t2_grouped[c - 1][:])
 
-        def step2(c):
-            acc = bank_out.tile([P, OUT_COLS], F32)
-            nc.tensor.matmul_mx(
-                out=acc[:],
-                lhsT=t2_codes[c][:].bitcast(FP8X4),
-                lhsT_scale=t2_scales[c][:],
-                rhs=codes3[:].bitcast(FP8X4),
-                rhs_scale=scales3[:],
-                start=True,
-                stop=True,
-            )
-            result = keep.tile([P, OUT_COLS], F32, name="result_%d" % c)
-            nc.scalar.copy(out=result[:], in_=acc[:])
-            for a in range(2):
-                nc.sync.dma_start(out=out_view[c // 2, c % 2, a], in_=result[:, a * 256 : (a + 1) * 256])
-
-        step1(0)
-        step1(1)
-        regroup(nc, grouped3, raw3)
-        quantise(nc, codes3, scales3, grouped3)
-        step2(0)
-        step2(1)
-        step1(2)
-        step2(2)
-        step1(3)
-        step2(3)
+        out_view = out.rearrange("(I i a) (O f) s -> i a O I (f s)", I=N_I, i=2, a=2, O=N_O)
+        accs = {}
+        for a in range(2):
+            cols = slice(a * HALF, (a + 1) * HALF)
+            quantise(nc, codes[PAIRS][:, cols], scales[PAIRS][:, cols], grouped[PAIRS][:, cols, :])
+            if a == 0:
+                regroup(nc, grouped[PAIRS], raw[PAIRS], HALF, HALF)
+                quantise(nc, t2_codes[PAIRS - 1][:], t2_scales[PAIRS - 1][:], t2_grouped[PAIRS - 1][:])
+            for c in range(PAIRS):
+                accs[c, a] = bank_out.tile([P, HALF], F32, name="acc")
+                nc.tensor.matmul_mx(
+                    out=accs[c, a][:],
+                    lhsT=t2_codes[c][:].bitcast(FP8X4),
+                    lhsT_scale=t2_scales[c][:],
+                    rhs=codes[PAIRS][:, cols].bitcast(FP8X4),
+                    rhs_scale=scales[PAIRS][:, cols],
+                    start=True,
+                    stop=True,
+                )
+        for a in range(2):
+            for i in range(2):
+                result = keep.tile([P, 2, HALF], F32, name="result_%d%d" % (i, a))
+                nc.vector.tensor_copy(out=result[:, 0, :], in_=accs[2 * i, a][:])
+                nc.scalar.copy(out=result[:, 1, :], in_=accs[2 * i + 1, a][:])
+                nc.sync.dma_start(out=out_view[i, a], in_=result[:].rearrange("p o f -> p (o f)"))

@@ -22,16 +22,11 @@ VECTOR_EIGHTHS = 6
 HALF = 256
 
 
-def regroup(nc, grouped, raw, first, count):
-    split = first + count * VECTOR_EIGHTHS // 8
-    for copy, cols in (
-        (nc.vector.tensor_copy, slice(first, split)),
-        (nc.scalar.copy, slice(split, first + count)),
-    ):
-        copy(
-            out=grouped[:, cols, :].rearrange("p (c n) j -> p c j n", n=4),
-            in_=raw[:, :, cols].rearrange("p j (c n) -> p c j n", n=4),
-        )
+def regroup(copy, grouped, raw, cols):
+    copy(
+        out=grouped[:, cols, :].rearrange("p (c n) j -> p c j n", n=4),
+        in_=raw[:, :, cols].rearrange("p j (c n) -> p c j n", n=4),
+    )
 
 
 def quantise(nc, codes, scales, grouped):
@@ -55,7 +50,9 @@ def tile_linear2mpo_pa_s_kernel(tc, t1, core2, core3, out):
         t1_rows = keep.tile([P, BOND], BF16)
         nc.scalar.dma_start(out=t1_rows[:], in_=t1.rearrange("i o r -> (i o) r"))
         raw = [keep.tile([P, PACK, BOND], BF16, name="raw_%d" % c) for c in range(PAIRS + 1)]
-        for c in range(PAIRS):
+        for cols in (slice(0, HALF), slice(HALF, BOND)):
+            nc.sync.dma_start(out=raw[0][:, :, cols], in_=core2_view[0][:, :, cols])
+        for c in range(1, PAIRS):
             nc.sync.dma_start(out=raw[c][:], in_=core2_view[c])
         nc.sync.dma_start(out=raw[PAIRS][:], in_=core3_view)
 
@@ -71,7 +68,25 @@ def tile_linear2mpo_pa_s_kernel(tc, t1, core2, core3, out):
         t2_codes = [keep.tile([P, P], U32, name="t2_codes_%d" % c, align_bytes=64) for c in range(PAIRS)]
         t2_scales = [keep.tile([P, P], U8, name="t2_scales_%d" % c, align_bytes=64) for c in range(PAIRS)]
 
-        regroup(nc, grouped[0], raw[0], 0, BOND)
+        pieces = [(0, 0, HALF), (0, HALF, HALF)] + [(c, 0, BOND) for c in range(1, PAIRS)]
+        pieces += [(PAIRS, 0, HALF), (PAIRS, HALF, HALF)]
+
+        def regroup_on_vector(n):
+            if n < len(pieces):
+                c, first, count = pieces[n]
+                split = first + count * VECTOR_EIGHTHS // 8
+                regroup(nc.vector.tensor_copy, grouped[c], raw[c], slice(first, split))
+
+        def regroup_on_scalar(n):
+            if n < len(pieces):
+                c, first, count = pieces[n]
+                split = first + count * VECTOR_EIGHTHS // 8
+                regroup(nc.scalar.copy, grouped[c], raw[c], slice(split, first + count))
+
+        FIRST = 2
+        for n in range(FIRST):
+            regroup_on_vector(n)
+            regroup_on_scalar(n)
 
         identity = keep.tile([P, P], F32)
         make_identity(nc, identity[:])
@@ -89,6 +104,7 @@ def tile_linear2mpo_pa_s_kernel(tc, t1, core2, core3, out):
         )
         t1_codes = keep.tile([P, P], U32, align_bytes=64)
         t1_scales = keep.tile([P, P], U8, align_bytes=64)
+        regroup_on_scalar(FIRST)
 
         for c in range(PAIRS):
             quantise(nc, codes[c][:], scales[c][:], grouped[c][:])
@@ -106,7 +122,8 @@ def tile_linear2mpo_pa_s_kernel(tc, t1, core2, core3, out):
                     start=True,
                     stop=True,
                 )
-            regroup(nc, grouped[c + 1], raw[c + 1], 0, BOND if c + 1 < PAIRS else HALF)
+            regroup_on_vector(FIRST + c)
+            regroup_on_scalar(FIRST + c + 1)
             nc.scalar.copy(out=t2_grouped[c][:], in_=t2_T[:].rearrange("p t w -> p w t"))
             if c > 0:
                 quantise(nc, t2_codes[c - 1][:], t2_scales[c - 1][:], t2_grouped[c - 1][:])
@@ -117,7 +134,7 @@ def tile_linear2mpo_pa_s_kernel(tc, t1, core2, core3, out):
             cols = slice(a * HALF, (a + 1) * HALF)
             quantise(nc, codes[PAIRS][:, cols], scales[PAIRS][:, cols], grouped[PAIRS][:, cols, :])
             if a == 0:
-                regroup(nc, grouped[PAIRS], raw[PAIRS], HALF, HALF)
+                regroup_on_vector(FIRST + PAIRS)
                 quantise(nc, t2_codes[PAIRS - 1][:], t2_scales[PAIRS - 1][:], t2_grouped[PAIRS - 1][:])
             for c in range(PAIRS):
                 accs[c, a] = bank_out.tile([P, HALF], F32, name="acc")

@@ -18,7 +18,7 @@ OUT_COLS = 512
 
 FLOPS = 2 * 128 * 512 * 2048 + 2 * 512 * 512 * 512
 
-VECTOR_EIGHTHS = 6
+VECTOR_EIGHTHS = 5
 HALF = 256
 
 

@@ -122,6 +122,9 @@ def tile_linear2mpo_pa_s_kernel(tc, t1, core2, core3, out):
                     start=True,
                     stop=True,
                 )
+            if c > 0:
+                warm = bank_out.tile([P, BOND], F32, name="acc", tag="acc")
+                nc.tensor.matmul(warm[:], lhsT=raw[0][:, 0, :P], rhs=raw[0][:, 1, :], start=True, stop=True)
             regroup_on_vector(FIRST + c)
             regroup_on_scalar(FIRST + c + 1)
             nc.scalar.copy(out=t2_grouped[c][:], in_=t2_T[:].rearrange("p t w -> p w t"))
@@ -137,7 +140,7 @@ def tile_linear2mpo_pa_s_kernel(tc, t1, core2, core3, out):
                 regroup_on_vector(FIRST + PAIRS)
                 quantise(nc, t2_codes[PAIRS - 1][:], t2_scales[PAIRS - 1][:], t2_grouped[PAIRS - 1][:])
             for c in range(PAIRS):
-                accs[c, a] = bank_out.tile([P, HALF], F32, name="acc")
+                accs[c, a] = bank_out.tile([P, HALF], F32, name="acc", tag="acc")
                 nc.tensor.matmul_mx(
                     out=accs[c, a][:],
                     lhsT=t2_codes[c][:].bitcast(FP8X4),

@@ -20,6 +20,7 @@ FLOPS = 2 * 128 * 512 * 2048 + 2 * 512 * 512 * 512
 
 VECTOR_EIGHTHS = 5
 HALF = 256
+CORE3 = PAIRS
 
 
 def regroup(copy, grouped, raw, cols):
@@ -48,13 +49,14 @@ def tile_linear2mpo_pa_s_kernel(tc, t1, core2, core3, out):
         core2_view = core2.rearrange("(p j) i o q -> (i o) p j q", j=PACK)
         core3_view = core3.rearrange("(t p) a b s -> p t (a b s)", p=P)
         t1_rows = keep.tile([P, BOND], BF16)
-        nc.scalar.dma_start(out=t1_rows[:], in_=t1.rearrange("i o r -> (i o) r"))
         raw = [keep.tile([P, PACK, BOND], BF16, name="raw_%d" % c) for c in range(PAIRS + 1)]
-        for cols in (slice(0, HALF), slice(HALF, BOND)):
-            nc.sync.dma_start(out=raw[0][:, :, cols], in_=core2_view[0][:, :, cols])
-        for c in range(1, PAIRS):
-            nc.sync.dma_start(out=raw[c][:], in_=core2_view[c])
-        nc.sync.dma_start(out=raw[PAIRS][:], in_=core3_view)
+        nc.scalar.dma_start(out=t1_rows[:], in_=t1.rearrange("i o r -> (i o) r"))
+        nc.sync.dma_start(out=raw[0][:, :, :HALF], in_=core2_view[0][:, :, :HALF])
+        nc.sync.dma_start(out=raw[0][:, :, HALF:], in_=core2_view[0][:, :, HALF:])
+        nc.sync.dma_start(out=raw[1][:], in_=core2_view[1])
+        nc.sync.dma_start(out=raw[2][:], in_=core2_view[2])
+        nc.sync.dma_start(out=raw[3][:], in_=core2_view[3])
+        nc.sync.dma_start(out=raw[CORE3][:], in_=core3_view)
 
         grouped = [
             keep.tile([P, BOND, PACK], BF16, name="grouped_%d" % c, align_bytes=64)
@@ -62,59 +64,54 @@ def tile_linear2mpo_pa_s_kernel(tc, t1, core2, core3, out):
         ]
         codes = [keep.tile([P, BOND], U32, name="codes_%d" % c, align_bytes=64) for c in range(PAIRS + 1)]
         scales = [keep.tile([P, BOND], U8, name="scales_%d" % c, align_bytes=64) for c in range(PAIRS + 1)]
-        t2_grouped = [
-            keep.tile([P, P, PACK], BF16, name="t2_grouped_%d" % c, align_bytes=64) for c in range(PAIRS)
-        ]
-        t2_codes = [keep.tile([P, P], U32, name="t2_codes_%d" % c, align_bytes=64) for c in range(PAIRS)]
-        t2_scales = [keep.tile([P, P], U8, name="t2_scales_%d" % c, align_bytes=64) for c in range(PAIRS)]
+        t2_grouped = keep.tile([P, PAIRS * P, PACK], BF16, align_bytes=64)
+        t2_codes = keep.tile([P, PAIRS * P], U32, align_bytes=64)
+        t2_scales = keep.tile([P, PAIRS * P], U8, align_bytes=64)
 
-        pieces = [(0, 0, HALF), (0, HALF, HALF)] + [(c, 0, BOND) for c in range(1, PAIRS)]
-        pieces += [(PAIRS, 0, HALF), (PAIRS, HALF, HALF)]
+        def regroup_on_vector(c, first, count):
+            split = first + count * VECTOR_EIGHTHS // 8
+            regroup(nc.vector.tensor_copy, grouped[c], raw[c], slice(first, split))
 
-        def regroup_on_vector(n):
-            if n < len(pieces):
-                c, first, count = pieces[n]
-                split = first + count * VECTOR_EIGHTHS // 8
-                regroup(nc.vector.tensor_copy, grouped[c], raw[c], slice(first, split))
+        def regroup_on_scalar(c, first, count):
+            split = first + count * VECTOR_EIGHTHS // 8
+            regroup(nc.scalar.copy, grouped[c], raw[c], slice(split, first + count))
 
-        def regroup_on_scalar(n):
-            if n < len(pieces):
-                c, first, count = pieces[n]
-                split = first + count * VECTOR_EIGHTHS // 8
-                regroup(nc.scalar.copy, grouped[c], raw[c], slice(split, first + count))
-
-        FIRST = 2
-        for n in range(FIRST):
-            regroup_on_vector(n)
-            regroup_on_scalar(n)
+        def quantise_columns(c, first, count):
+            cols = slice(first, first + count)
+            quantise(nc, codes[c][:, cols], scales[c][:, cols], grouped[c][:, cols, :])
 
         identity = keep.tile([P, P], F32)
         make_identity(nc, identity[:])
-        t1_words = t1_rows[:].bitcast(F32).rearrange("c (p u) -> c u p", u=2)
         t1_T = bank_t2.tile([P, 2, P], F32, tag="t2_T")
-        for u in range(2):
-            nc.tensor.transpose(t1_T[:, u, :], t1_words[:, u, :], identity[:])
         t1_grouped = keep.tile([P, P, PACK], BF16, align_bytes=64)
-        nc.scalar.copy(
-            out=t1_grouped[:]
-            .rearrange("p w j -> p (w j)")
-            .bitcast(F32)
-            .rearrange("p (o i u) -> p o i u", o=N_O, i=N_I),
-            in_=t1_T[:].rearrange("p u (i o) -> p o i u", i=N_I),
-        )
         t1_codes = keep.tile([P, P], U32, align_bytes=64)
         t1_scales = keep.tile([P, P], U8, align_bytes=64)
-        regroup_on_scalar(FIRST)
 
-        for c in range(PAIRS):
-            quantise(nc, codes[c][:], scales[c][:], grouped[c][:])
-            if c == 0:
-                quantise(nc, t1_codes[:], t1_scales[:], t1_grouped[:])
-            t2_T = bank_t2.tile([P, PACK, P], F32, tag="t2_T")
+        def transpose_t1():
+            t1_words = t1_rows[:].bitcast(F32).rearrange("c (p u) -> c u p", u=2)
+            for u in range(2):
+                nc.tensor.transpose(t1_T[:, u, :], t1_words[:, u, :], identity[:])
+
+        def group_t1():
+            nc.scalar.copy(
+                out=t1_grouped[:]
+                .rearrange("p w j -> p (w j)")
+                .bitcast(F32)
+                .rearrange("p (o i u) -> p o i u", o=N_O, i=N_I),
+                in_=t1_T[:].rearrange("p u (i o) -> p o i u", i=N_I),
+            )
+
+        def quantise_t1():
+            quantise(nc, t1_codes[:], t1_scales[:], t1_grouped[:])
+
+        t2_T = {}
+
+        def step_1(c):
+            t2_T[c] = bank_t2.tile([P, PACK, P], F32, tag="t2_T", name="t2_T")
             for t in range(PACK):
                 cols = slice(t * P, (t + 1) * P)
                 nc.tensor.matmul_mx(
-                    out=t2_T[:, t, :],
+                    out=t2_T[c][:, t, :],
                     lhsT=codes[c][:, cols].bitcast(FP8X4),
                     lhsT_scale=scales[c][:, cols],
                     rhs=t1_codes[:].bitcast(FP8X4),
@@ -122,37 +119,112 @@ def tile_linear2mpo_pa_s_kernel(tc, t1, core2, core3, out):
                     start=True,
                     stop=True,
                 )
-            if c > 0:
-                warm = bank_out.tile([P, BOND], F32, name="acc", tag="acc")
-                nc.tensor.matmul(warm[:], lhsT=raw[0][:, 0, :P], rhs=raw[0][:, 1, :], start=True, stop=True)
-            regroup_on_vector(FIRST + c)
-            regroup_on_scalar(FIRST + c + 1)
-            nc.scalar.copy(out=t2_grouped[c][:], in_=t2_T[:].rearrange("p t w -> p w t"))
-            if c > 0:
-                quantise(nc, t2_codes[c - 1][:], t2_scales[c - 1][:], t2_grouped[c - 1][:])
 
-        out_view = out.rearrange("(I i a) (O f) s -> i a O I (f s)", I=N_I, i=2, a=2, O=N_O)
+        def round_t2(copy, c):
+            copy(
+                out=t2_grouped[:, c * P : (c + 1) * P, :],
+                in_=t2_T[c][:].rearrange("p t w -> p w t"),
+            )
+
+        def quantise_t2(c, pairs=1):
+            cols = slice(c * P, (c + pairs) * P)
+            quantise(nc, t2_codes[:, cols], t2_scales[:, cols], t2_grouped[:, cols, :])
+
+        def idle_pass(c):
+            unread = bank_out.tile([P, BOND], F32, tag="acc", name="unread")
+            nc.tensor.matmul_mx(
+                out=unread[:],
+                lhsT=t1_codes[:].bitcast(FP8X4),
+                lhsT_scale=t1_scales[:],
+                rhs=codes[c][:].bitcast(FP8X4),
+                rhs_scale=scales[c][:],
+                start=True,
+                stop=True,
+            )
+
         accs = {}
-        for a in range(2):
+
+        def step_2(c, a):
             cols = slice(a * HALF, (a + 1) * HALF)
-            quantise(nc, codes[PAIRS][:, cols], scales[PAIRS][:, cols], grouped[PAIRS][:, cols, :])
-            if a == 0:
-                regroup_on_vector(FIRST + PAIRS)
-                quantise(nc, t2_codes[PAIRS - 1][:], t2_scales[PAIRS - 1][:], t2_grouped[PAIRS - 1][:])
-            for c in range(PAIRS):
-                accs[c, a] = bank_out.tile([P, HALF], F32, name="acc", tag="acc")
-                nc.tensor.matmul_mx(
-                    out=accs[c, a][:],
-                    lhsT=t2_codes[c][:].bitcast(FP8X4),
-                    lhsT_scale=t2_scales[c][:],
-                    rhs=codes[PAIRS][:, cols].bitcast(FP8X4),
-                    rhs_scale=scales[PAIRS][:, cols],
-                    start=True,
-                    stop=True,
-                )
-        for a in range(2):
-            for i in range(2):
-                result = keep.tile([P, 2, HALF], F32, name="result_%d%d" % (i, a))
-                nc.vector.tensor_copy(out=result[:, 0, :], in_=accs[2 * i, a][:])
-                nc.scalar.copy(out=result[:, 1, :], in_=accs[2 * i + 1, a][:])
-                nc.sync.dma_start(out=out_view[i, a], in_=result[:].rearrange("p o f -> p (o f)"))
+            accs[c, a] = bank_out.tile([P, HALF], F32, tag="acc", name="acc")
+            nc.tensor.matmul_mx(
+                out=accs[c, a][:],
+                lhsT=t2_codes[:, c * P : (c + 1) * P].bitcast(FP8X4),
+                lhsT_scale=t2_scales[:, c * P : (c + 1) * P],
+                rhs=codes[CORE3][:, cols].bitcast(FP8X4),
+                rhs_scale=scales[CORE3][:, cols],
+                start=True,
+                stop=True,
+            )
+
+        out_view = out.rearrange("(I i a) (O o b) s -> i a O I o (b s)", I=N_I, i=2, a=2, O=N_O, o=2)
+        results = [
+            [keep.tile([P, 2, HALF], F32, name="result_%d%d" % (i, a)) for a in range(2)] for i in range(2)
+        ]
+
+        def empty_bank(copy, c, a):
+            copy(out=results[c // 2][a][:, c % 2, :], in_=accs[c, a][:])
+
+        def store(i, a):
+            nc.sync.dma_start(
+                out=out_view[i, a].rearrange("O I o f -> O I (o f)"),
+                in_=results[i][a][:].rearrange("p o f -> p (o f)"),
+            )
+
+        regroup_on_vector(0, 0, HALF)
+        regroup_on_scalar(0, 0, HALF)
+        regroup_on_vector(0, HALF, HALF)
+        regroup_on_scalar(0, HALF, HALF)
+        transpose_t1()
+        group_t1()
+        regroup_on_scalar(1, 0, BOND)
+        quantise_columns(0, 0, BOND)
+        quantise_t1()
+        step_1(0)
+        idle_pass(0)
+        regroup_on_vector(1, 0, BOND)
+        regroup_on_scalar(2, 0, BOND)
+        round_t2(nc.scalar.copy, 0)
+        regroup_on_vector(2, 0, BOND)
+        quantise_columns(1, 0, BOND)
+        step_1(1)
+        idle_pass(1)
+        regroup_on_scalar(3, 0, BOND)
+        round_t2(nc.scalar.copy, 1)
+        regroup_on_vector(3, 0, BOND)
+        quantise_columns(2, 0, BOND)
+        step_1(2)
+        idle_pass(2)
+        regroup_on_scalar(CORE3, 0, HALF)
+        round_t2(nc.scalar.copy, 2)
+        regroup_on_vector(CORE3, 0, HALF)
+        quantise_columns(3, 0, BOND)
+        step_1(3)
+        idle_pass(3)
+        regroup_on_scalar(CORE3, HALF, HALF)
+        quantise_t2(0, 2)
+        regroup_on_vector(CORE3, HALF, HALF)
+        round_t2(nc.scalar.copy, 3)
+        quantise_columns(CORE3, 0, HALF)
+        step_2(0, 0)
+        step_2(1, 0)
+        empty_bank(nc.scalar.copy, 0, 0)
+        empty_bank(nc.scalar.copy, 1, 0)
+        store(0, 0)
+        quantise_columns(CORE3, HALF, HALF)
+        step_2(0, 1)
+        step_2(1, 1)
+        quantise_t2(2, 2)
+        step_2(2, 0)
+        step_2(3, 0)
+        step_2(2, 1)
+        step_2(3, 1)
+        empty_bank(nc.vector.tensor_copy, 0, 1)
+        empty_bank(nc.scalar.copy, 1, 1)
+        store(0, 1)
+        empty_bank(nc.vector.tensor_copy, 2, 0)
+        empty_bank(nc.scalar.copy, 3, 0)
+        store(1, 0)
+        empty_bank(nc.vector.tensor_copy, 2, 1)
+        empty_bank(nc.scalar.copy, 3, 1)
+        store(1, 1)

@@ -50,9 +50,8 @@ def tile_linear2mpo_pa_s_kernel(tc, t1, core2, core3, out):
         core3_view = core3.rearrange("(t p) a b s -> p t (a b s)", p=P)
         t1_rows = keep.tile([P, BOND], BF16)
         raw = [keep.tile([P, PACK, BOND], BF16, name="raw_%d" % c) for c in range(PAIRS + 1)]
-        nc.scalar.dma_start(out=t1_rows[:], in_=t1.rearrange("i o r -> (i o) r"))
-        nc.sync.dma_start(out=raw[0][:, :, :HALF], in_=core2_view[0][:, :, :HALF])
-        nc.sync.dma_start(out=raw[0][:, :, HALF:], in_=core2_view[0][:, :, HALF:])
+        nc.sync.dma_start(out=raw[0][:], in_=core2_view[0])
+        nc.sync.dma_start(out=t1_rows[:], in_=t1.rearrange("i o r -> (i o) r"))
         nc.sync.dma_start(out=raw[1][:], in_=core2_view[1])
         nc.sync.dma_start(out=raw[2][:], in_=core2_view[2])
         nc.sync.dma_start(out=raw[3][:], in_=core2_view[3])
@@ -178,7 +177,8 @@ def tile_linear2mpo_pa_s_kernel(tc, t1, core2, core3, out):
         transpose_t1()
         group_t1()
         regroup_on_scalar(1, 0, BOND)
-        quantise_columns(0, 0, BOND)
+        quantise_columns(0, 0, HALF)
+        quantise_columns(0, HALF, HALF)
         quantise_t1()
         step_1(0)
         idle_pass(0)

@@ -202,12 +202,12 @@ def tile_linear2mpo_pa_s_kernel(tc, t1, core2, core3, out):
         step_1(3)
         idle_pass(3)
         regroup_on_scalar(CORE3, HALF, HALF)
-        quantise_t2(0, 2)
-        regroup_on_vector(CORE3, HALF, HALF)
-        round_t2(nc.scalar.copy, 3)
         quantise_columns(CORE3, 0, HALF)
+        quantise_t2(0, 2)
         step_2(0, 0)
         step_2(1, 0)
+        regroup_on_vector(CORE3, HALF, HALF)
+        round_t2(nc.scalar.copy, 3)
         empty_bank(nc.scalar.copy, 0, 0)
         empty_bank(nc.scalar.copy, 1, 0)
         store(0, 0)

@@ -53,9 +53,10 @@ def tile_linear2mpo_pa_s_kernel(tc, t1, core2, core3, out):
         nc.sync.dma_start(out=raw[0][:], in_=core2_view[0])
         nc.sync.dma_start(out=t1_rows[:], in_=t1.rearrange("i o r -> (i o) r"))
         nc.sync.dma_start(out=raw[1][:], in_=core2_view[1])
+        nc.sync.dma_start(out=raw[CORE3][:, :, :HALF], in_=core3_view[:, :, :HALF])
         nc.sync.dma_start(out=raw[2][:], in_=core2_view[2])
         nc.sync.dma_start(out=raw[3][:], in_=core2_view[3])
-        nc.sync.dma_start(out=raw[CORE3][:], in_=core3_view)
+        nc.sync.dma_start(out=raw[CORE3][:, :, HALF:], in_=core3_view[:, :, HALF:])
 
         grouped = [
             keep.tile([P, BOND, PACK], BF16, name="grouped_%d" % c, align_bytes=64)
@@ -170,6 +171,9 @@ def tile_linear2mpo_pa_s_kernel(tc, t1, core2, core3, out):
                 in_=results[i][a][:].rearrange("p o f -> p (o f)"),
             )
 
+        def store_one(queue, c, a):
+            queue.dma_start(out=out_view[c // 2, a][:, :, c % 2, :], in_=results[c // 2][a][:, c % 2, :])
+
         regroup_on_vector(0, 0, HALF)
         regroup_on_scalar(0, 0, HALF)
         regroup_on_vector(0, HALF, HALF)
@@ -183,48 +187,51 @@ def tile_linear2mpo_pa_s_kernel(tc, t1, core2, core3, out):
         step_1(0)
         idle_pass(0)
         regroup_on_vector(1, 0, BOND)
-        regroup_on_scalar(2, 0, BOND)
         round_t2(nc.scalar.copy, 0)
-        regroup_on_vector(2, 0, BOND)
+        regroup_on_scalar(CORE3, 0, HALF)
+        regroup_on_vector(CORE3, 0, HALF)
         quantise_columns(1, 0, BOND)
         step_1(1)
         idle_pass(1)
-        regroup_on_scalar(3, 0, BOND)
+        quantise_t2(0)
+        regroup_on_scalar(2, 0, BOND)
+        regroup_on_vector(2, 0, BOND)
+        quantise_columns(CORE3, 0, HALF)
+        step_2(0, 0)
         round_t2(nc.scalar.copy, 1)
-        regroup_on_vector(3, 0, BOND)
         quantise_columns(2, 0, BOND)
         step_1(2)
         idle_pass(2)
-        regroup_on_scalar(CORE3, 0, HALF)
-        round_t2(nc.scalar.copy, 2)
-        regroup_on_vector(CORE3, 0, HALF)
+        regroup_on_scalar(3, 0, BOND)
+        regroup_on_vector(3, 0, BOND)
+        quantise_t2(1)
+        step_2(1, 0)
         quantise_columns(3, 0, BOND)
         step_1(3)
         idle_pass(3)
         regroup_on_scalar(CORE3, HALF, HALF)
-        quantise_columns(CORE3, 0, HALF)
-        quantise_t2(0, 2)
-        step_2(0, 0)
-        step_2(1, 0)
         regroup_on_vector(CORE3, HALF, HALF)
-        round_t2(nc.scalar.copy, 3)
+        round_t2(nc.scalar.copy, 2)
         empty_bank(nc.scalar.copy, 0, 0)
         empty_bank(nc.scalar.copy, 1, 0)
         store(0, 0)
+        quantise_t2(2)
+        step_2(2, 0)
         quantise_columns(CORE3, HALF, HALF)
         step_2(0, 1)
         step_2(1, 1)
-        quantise_t2(2, 2)
-        step_2(2, 0)
-        step_2(3, 0)
         step_2(2, 1)
-        step_2(3, 1)
-        empty_bank(nc.vector.tensor_copy, 0, 1)
-        empty_bank(nc.scalar.copy, 1, 1)
-        store(0, 1)
+        round_t2(nc.scalar.copy, 3)
         empty_bank(nc.vector.tensor_copy, 2, 0)
-        empty_bank(nc.scalar.copy, 3, 0)
-        store(1, 0)
+        store_one(nc.sync, 2, 0)
+        quantise_t2(3)
+        step_2(3, 0)
+        step_2(3, 1)
+        empty_bank(nc.scalar.copy, 1, 1)
+        empty_bank(nc.vector.tensor_copy, 0, 1)
+        store(0, 1)
         empty_bank(nc.vector.tensor_copy, 2, 1)
-        empty_bank(nc.scalar.copy, 3, 1)
+        empty_bank(nc.scalar.copy, 3, 0)
+        store_one(nc.sync, 3, 0)
+        empty_bank(nc.vector.tensor_copy, 3, 1)
         store(1, 1)

from contextlib import ExitStack

import concourse.mybir as mybir
from concourse.masks import make_identity

BF16 = mybir.dt.bfloat16
F32 = mybir.dt.float32
U32 = mybir.dt.uint32
U8 = mybir.dt.uint8
FP8X4 = mybir.dt.float8_e4m3fn_x4

P = 128
PACK = 4
BOND = P * PACK
N_I, N_O = 8, 16
PAIRS = 4
OUT_COLS = 512

FLOPS = 2 * 128 * 512 * 2048 + 2 * 512 * 512 * 512

VECTOR_EIGHTHS = 5
HALF = 256
CORE3 = PAIRS


def regroup(copy, grouped, raw, cols):
    copy(
        out=grouped[:, cols, :].rearrange("p (c n) j -> p c j n", n=4),
        in_=raw[:, :, cols].rearrange("p j (c n) -> p c j n", n=4),
    )


def quantise(nc, codes, scales, grouped):
    nc.vector.quantize_mx(
        out=codes.bitcast(FP8X4),
        scales=scales,
        in_=grouped.rearrange("p w j -> p (w j)"),
    )


def tile_linear2mpo_pa_s_kernel(tc, t1, core2, core3, out):
    nc = tc.nc
    with ExitStack() as ctx:
        ctx.enter_context(tc.manual_schedule())
        keep = ctx.enter_context(tc.tile_pool(name="keep", bufs=1))
        bank_t2 = ctx.enter_context(tc.psum_pool(name="bank_t2", bufs=2))
        bank_out = ctx.enter_context(tc.psum_pool(name="bank_out", bufs=6))

        core2_view = core2.rearrange("(p j) i o q -> (i o) p j q", j=PACK)
        core3_view = core3.rearrange("(t p) a b s -> p t (a b s)", p=P)
        t1_rows = keep.tile([P, BOND], BF16)
        raw = [keep.tile([P, PACK, BOND], BF16, name="raw_%d" % c) for c in range(PAIRS + 1)]
        nc.sync.dma_start(out=raw[0][:], in_=core2_view[0])
        nc.sync.dma_start(out=t1_rows[:], in_=t1.rearrange("i o r -> (i o) r"))
        nc.sync.dma_start(out=raw[1][:], in_=core2_view[1])
        nc.sync.dma_start(out=raw[CORE3][:, :, :HALF], in_=core3_view[:, :, :HALF])
        nc.sync.dma_start(out=raw[2][:], in_=core2_view[2])
        nc.sync.dma_start(out=raw[3][:], in_=core2_view[3])
        nc.sync.dma_start(out=raw[CORE3][:, :, HALF:], in_=core3_view[:, :, HALF:])

        grouped = [
            keep.tile([P, BOND, PACK], BF16, name="grouped_%d" % c, align_bytes=64)
            for c in range(PAIRS + 1)
        ]
        codes = [keep.tile([P, BOND], U32, name="codes_%d" % c, align_bytes=64) for c in range(PAIRS + 1)]
        scales = [keep.tile([P, BOND], U8, name="scales_%d" % c, align_bytes=64) for c in range(PAIRS + 1)]
        t2_grouped = keep.tile([P, PAIRS * P, PACK], BF16, align_bytes=64)
        t2_codes = keep.tile([P, PAIRS * P], U32, align_bytes=64)
        t2_scales = keep.tile([P, PAIRS * P], U8, align_bytes=64)

        def regroup_on_vector(c, first, count):
            split = first + count * VECTOR_EIGHTHS // 8
            regroup(nc.vector.tensor_copy, grouped[c], raw[c], slice(first, split))

        def regroup_on_scalar(c, first, count):
            split = first + count * VECTOR_EIGHTHS // 8
            regroup(nc.scalar.copy, grouped[c], raw[c], slice(split, first + count))

        def quantise_columns(c, first, count):
            cols = slice(first, first + count)
            quantise(nc, codes[c][:, cols], scales[c][:, cols], grouped[c][:, cols, :])

        identity = keep.tile([P, P], F32)
        make_identity(nc, identity[:])
        t1_T = bank_t2.tile([P, 2, P], F32, tag="t2_T")
        t1_grouped = keep.tile([P, P, PACK], BF16, align_bytes=64)
        t1_codes = keep.tile([P, P], U32, align_bytes=64)
        t1_scales = keep.tile([P, P], U8, align_bytes=64)

        def transpose_t1():
            t1_words = t1_rows[:].bitcast(F32).rearrange("c (p u) -> c u p", u=2)
            for u in range(2):
                nc.tensor.transpose(t1_T[:, u, :], t1_words[:, u, :], identity[:])

        def group_t1():
            nc.scalar.copy(
                out=t1_grouped[:]
                .rearrange("p w j -> p (w j)")
                .bitcast(F32)
                .rearrange("p (o i u) -> p o i u", o=N_O, i=N_I),
                in_=t1_T[:].rearrange("p u (i o) -> p o i u", i=N_I),
            )

        def quantise_t1():
            quantise(nc, t1_codes[:], t1_scales[:], t1_grouped[:])

        t2_T = {}

        def step_1(c):
            t2_T[c] = bank_t2.tile([P, PACK, P], F32, tag="t2_T", name="t2_T")
            for t in range(PACK):
                cols = slice(t * P, (t + 1) * P)
                nc.tensor.matmul_mx(
                    out=t2_T[c][:, t, :],
                    lhsT=codes[c][:, cols].bitcast(FP8X4),
                    lhsT_scale=scales[c][:, cols],
                    rhs=t1_codes[:].bitcast(FP8X4),
                    rhs_scale=t1_scales[:],
                    start=True,
                    stop=True,
                )

        def round_t2(copy, c):
            copy(
                out=t2_grouped[:, c * P : (c + 1) * P, :],
                in_=t2_T[c][:].rearrange("p t w -> p w t"),
            )

        def quantise_t2(c, pairs=1):
            cols = slice(c * P, (c + pairs) * P)
            quantise(nc, t2_codes[:, cols], t2_scales[:, cols], t2_grouped[:, cols, :])

        def idle_pass(c):
            unread = bank_out.tile([P, BOND], F32, tag="acc", name="unread")
            nc.tensor.matmul_mx(
                out=unread[:],
                lhsT=t1_codes[:].bitcast(FP8X4),
                lhsT_scale=t1_scales[:],
                rhs=codes[c][:].bitcast(FP8X4),
                rhs_scale=scales[c][:],
                start=True,
                stop=True,
            )

        accs = {}

        def step_2(c, a):
            cols = slice(a * HALF, (a + 1) * HALF)
            accs[c, a] = bank_out.tile([P, HALF], F32, tag="acc", name="acc")
            nc.tensor.matmul_mx(
                out=accs[c, a][:],
                lhsT=t2_codes[:, c * P : (c + 1) * P].bitcast(FP8X4),
                lhsT_scale=t2_scales[:, c * P : (c + 1) * P],
                rhs=codes[CORE3][:, cols].bitcast(FP8X4),
                rhs_scale=scales[CORE3][:, cols],
                start=True,
                stop=True,
            )

        out_view = out.rearrange("(I i a) (O o b) s -> i a O I o (b s)", I=N_I, i=2, a=2, O=N_O, o=2)
        results = [
            [keep.tile([P, 2, HALF], F32, name="result_%d%d" % (i, a)) for a in range(2)] for i in range(2)
        ]

        def empty_bank(copy, c, a):
            copy(out=results[c // 2][a][:, c % 2, :], in_=accs[c, a][:])

        def store(i, a):
            nc.sync.dma_start(
                out=out_view[i, a].rearrange("O I o f -> O I (o f)"),
                in_=results[i][a][:].rearrange("p o f -> p (o f)"),
            )

        def store_one(queue, c, a):
            queue.dma_start(out=out_view[c // 2, a][:, :, c % 2, :], in_=results[c // 2][a][:, c % 2, :])

        regroup_on_vector(0, 0, HALF)
        regroup_on_scalar(0, 0, HALF)
        regroup_on_vector(0, HALF, HALF)
        regroup_on_scalar(0, HALF, HALF)
        transpose_t1()
        group_t1()
        regroup_on_scalar(1, 0, BOND)
        quantise_columns(0, 0, HALF)
        quantise_columns(0, HALF, HALF)
        quantise_t1()
        step_1(0)
        idle_pass(0)
        regroup_on_vector(1, 0, BOND)
        round_t2(nc.scalar.copy, 0)
        regroup_on_scalar(CORE3, 0, HALF)
        regroup_on_vector(CORE3, 0, HALF)
        quantise_columns(1, 0, BOND)
        step_1(1)
        idle_pass(1)
        quantise_t2(0)
        regroup_on_scalar(2, 0, BOND)
        regroup_on_vector(2, 0, BOND)
        quantise_columns(CORE3, 0, HALF)
        step_2(0, 0)
        round_t2(nc.scalar.copy, 1)
        quantise_columns(2, 0, BOND)
        step_1(2)
        idle_pass(2)
        regroup_on_scalar(3, 0, BOND)
        regroup_on_vector(3, 0, BOND)
        quantise_t2(1)
        step_2(1, 0)
        quantise_columns(3, 0, BOND)
        step_1(3)
        idle_pass(3)
        regroup_on_scalar(CORE3, HALF, HALF)
        regroup_on_vector(CORE3, HALF, HALF)
        round_t2(nc.scalar.copy, 2)
        empty_bank(nc.scalar.copy, 0, 0)
        empty_bank(nc.scalar.copy, 1, 0)
        store(0, 0)
        quantise_t2(2)
        step_2(2, 0)
        quantise_columns(CORE3, HALF, HALF)
        step_2(0, 1)
        step_2(1, 1)
        step_2(2, 1)
        round_t2(nc.scalar.copy, 3)
        empty_bank(nc.vector.tensor_copy, 2, 0)
        store_one(nc.sync, 2, 0)
        quantise_t2(3)
        step_2(3, 0)
        step_2(3, 1)
        empty_bank(nc.scalar.copy, 1, 1)
        empty_bank(nc.vector.tensor_copy, 0, 1)
        store(0, 1)
        empty_bank(nc.vector.tensor_copy, 2, 1)
        empty_bank(nc.scalar.copy, 3, 0)
        store_one(nc.sync, 3, 0)
        empty_bank(nc.vector.tensor_copy, 3, 1)
        store(1, 1)
